import numpy as np
import ml_dtypes


def mxq(x, axis, fmt="e4m3"):
    dtype, down = {"e4m3": (ml_dtypes.float8_e4m3fn, 7), "e5m2": (ml_dtypes.float8_e5m2, 14)}[fmt]
    v = np.moveaxis(np.asarray(x, np.float32).astype(ml_dtypes.bfloat16).astype(np.float64), axis, -1)
    blocks = v.reshape(v.shape[:-1] + (-1, 32))
    amax = np.abs(blocks).max(-1, keepdims=True)
    byte = np.maximum(np.where(amax > 0, np.frexp(amax)[1] - 1 + 127, 0) - down, 1)
    scale = np.exp2(byte - 127.0)
    codes = (blocks / scale).astype(np.float32).astype(dtype).astype(np.float64)
    return np.moveaxis((codes * scale).reshape(v.shape), -1, axis)


WIDE = False


def mx_kscale(k):
    if not WIDE:
        return np.ones(k)
    levels = np.array([10, -10, 5, -5, 0])
    a = np.random.permutation(np.resize(levels, k // 512 * 4)).reshape(k // 512, 4)
    idx = np.arange(k)
    return np.exp2(a[idx // 512, idx % 128 // 32])


BF16 = ml_dtypes.bfloat16


def bf(x):
    return np.asarray(x, np.float32).astype(BF16)


def f64(x):
    return np.asarray(x).astype(np.float64)


E2M1 = np.array([0.0, 0.5, 1.0, 1.5, 2.0, 3.0, 4.0, 6.0, -0.0, -0.5, -1.0, -1.5, -2.0, -3.0, -4.0, -6.0])


def pack_weight(w, fmt):
    k, n = w.shape
    w = f64(bf(w)).reshape(k // 32, 32, n)
    amax = np.abs(w).max(1)
    if fmt == "e4m3":
        byte = np.frexp(amax)[1] - 1 + 127 - 7
    else:
        mant, ex = np.frexp(amax / 6.0)
        byte = np.where(mant > 0.5, ex, ex - 1) + 127
    byte = np.clip(np.where(amax > 0, byte, 1), 1, 254)
    scaled = (w * np.exp2(127.0 - byte)[:, None, :]).reshape(k, n).astype(np.float32)
    by_word = np.ascontiguousarray(scaled.reshape(k // 512, 128, 4, n).transpose(0, 1, 3, 2))
    if fmt == "e4m3":
        words = by_word.astype(ml_dtypes.float8_e4m3fn).view(np.uint8)
    else:
        c = by_word.astype(ml_dtypes.float4_e2m1fn).view(np.uint8) & 0xF
        words = c[..., 0::2] | (c[..., 1::2] << 4)
    return np.ascontiguousarray(words), np.ascontiguousarray(byte.astype(np.uint8).reshape(k // 512, 16, n))


def unpack_weight(words, scales, fmt):
    g, p, n, _ = words.shape
    if fmt == "e4m3":
        vals = np.ascontiguousarray(words).view(ml_dtypes.float8_e4m3fn).astype(np.float64)
    else:
        nib = np.empty((g, p, n, 4), np.uint8)
        nib[..., 0::2] = words & 0xF
        nib[..., 1::2] = words >> 4
        vals = E2M1[nib]
    vals = vals * np.repeat(np.exp2(scales.astype(np.float64) - 127.0), 8, axis=1)[..., None]
    return vals.transpose(0, 1, 3, 2).reshape(g * 512, n)


B, S, D, H, KVH, DH, F = 2, 64, 8192, 8, 2, 128, 2048
EPS = 1e-6
E = H * DH


def rms_norm(v, eps):
    return v / np.sqrt(np.mean(np.square(v), axis=-1, keepdims=True) + eps)


def setup_inputs():
    s = mx_kscale(E)
    y_attn = bf(np.random.standard_normal((B, H, S, DH)) * 0.35 * s.reshape(H, 1, DH))
    x = bf(np.random.standard_normal((B, S, D)))
    w_o = np.random.standard_normal((D, E)) / np.sqrt(E) / s[None, :]
    attn_scale = bf(1.0 + 0.1 * np.random.standard_normal(D))
    w_fc = np.random.standard_normal((F, D)) / np.sqrt(D)
    w_o_words, w_o_scales = pack_weight(np.ascontiguousarray(w_o.T), "e4m3")
    w_fc_words, w_fc_scales = pack_weight(np.ascontiguousarray(w_fc.T), "e4m3")
    return {"y_attn": y_attn,
            "x": x,
            "w_o_words": w_o_words,
            "w_o_scales": w_o_scales,
            "attn_scale": attn_scale,
            "w_fc_words": w_fc_words,
            "w_fc_scales": w_fc_scales}


def reference(y_attn, x, w_o_words, w_o_scales, attn_scale, w_fc_words, w_fc_scales):
    yc = f64(y_attn).transpose(0, 2, 1, 3).reshape(B, S, E)
    attn_out = mxq(yc, 2, "e4m3") @ unpack_weight(w_o_words, w_o_scales, "e4m3")
    x_mid = f64(x) + f64(attn_scale)[None, None, :] * attn_out
    h = mxq(rms_norm(x_mid, EPS), 2, "e4m3") @ unpack_weight(w_fc_words, w_fc_scales, "e4m3")
    h = np.square(np.maximum(h, 0.0))
    return x_mid, h

@@ -1,0 +1,269 @@
+import concourse.mybir as mybir
+from concourse.masks import make_identity
+
+F32 = mybir.dt.float32
+BF16 = mybir.dt.bfloat16
+I32 = mybir.dt.int32
+U32 = mybir.dt.uint32
+U8 = mybir.dt.uint8
+FP8X4 = mybir.dt.float8_e4m3fn_x4
+ACT = mybir.ActivationFunctionType
+ALU = mybir.AluOpType
+
+P = 128
+HEADS = 8
+HEAD_DIM = 128
+E = HEADS * HEAD_DIM
+D = 8192
+F = 2048
+EPS = 1e-6
+
+K_PASS = 512
+BANK = 512
+CHUNK = 2048
+BANKS_PER_CHUNK = CHUNK // BANK
+WO_GROUPS = E // K_PASS
+FC_GROUPS = D // K_PASS
+WO_BLOCKS = D // CHUNK
+PAIR = 2 * K_PASS
+PLANES_PER_TILE = 4
+QUADRANT = 32
+WEIGHT_SLOTS = 16
+
+FLOPS = 2 * P * E * D + 2 * P * D * F
+
+
+def load_chunk(nc, weights, words):
+    chunk = weights.tile([P, CHUNK], U32, tag="chunk", align_bytes=64)
+    nc.sync.dma_start(out=chunk[:].bitcast(I32), in_=words)
+    return chunk
+
+
+def load_scale_planes(nc, planes, rows):
+    for quad in range(P // QUADRANT):
+        nc.sync.dma_start(
+            out=planes[QUADRANT * quad : QUADRANT * quad + 16, :].bitcast(I32),
+            in_=rows[:, 4 * quad : 4 * quad + 4, :],
+        )
+
+
+def transpose_pair(nc, bank, identity, tokens_by_k, grouped):
+    words = tokens_by_k.bitcast(F32)
+    half = K_PASS // 2
+    flipped = bank.rearrange("p (g u m) -> p g u m", g=2, u=2)
+    for g in range(2):
+        for u in range(2):
+            nc.tensor.transpose(
+                flipped[:, g, u, :], words[:, half * g + u : half * (g + 1) : 2], identity
+            )
+    nc.scalar.copy(
+        out=grouped.bitcast(F32).rearrange("p (g m u) -> p g m u", g=2, u=2),
+        in_=flipped.rearrange("p g u m -> p g m u"),
+    )
+
+
+def tile_shepherdembryo_pb_k_kernel(
+    tc, y_attn, x, w_o_words, w_o_scales, attn_scale, w_fc_words, w_fc_scales, out_0, out_1
+):
+    nc = tc.nc
+    x_rows = x.rearrange("b s d -> (b s) d")
+    x_mid_rows = out_0.rearrange("b s d -> (b s) d")
+    h_rows = out_1.rearrange("b s f -> (b s) f")
+    wo_words = w_o_words.rearrange("g p n t -> g p (n t)").bitcast(I32)
+    fc_words = w_fc_words.rearrange("g p n t -> g p (n t)").bitcast(I32)
+    wo_scale_rows = w_o_scales.bitcast(I32)
+    fc_scale_rows = w_fc_scales.bitcast(I32)
+
+    with tc.manual_schedule(), tc.tile_pool(name="keep", bufs=1) as keep, tc.tile_pool(
+        name="weights", bufs=WEIGHT_SLOTS
+    ) as weights:
+        identity_f32 = keep.tile([P, P], F32)
+        x_mid = keep.tile([P, D], F32)
+        sum_squares = keep.tile([P, D // BANK], F32)
+        fc_planes = keep.tile([P, (FC_GROUPS // PLANES_PER_TILE) * F], U8, align_bytes=64)
+
+        with tc.tile_pool(name="first", bufs=1) as first, tc.tile_pool(
+            name="scratch", bufs=2
+        ) as scratch, tc.psum_pool(name="banks", bufs=8) as banks:
+            one = first.tile([P, 1], F32)
+            identity_bf16 = first.tile([P, P], BF16)
+            gain_rows = first.tile([P, BANK], BF16)
+            gain = first.tile([P, D], BF16)
+            x_sb = first.tile([P, D], BF16)
+            wo_planes = first.tile([P, WO_GROUPS * CHUNK], U8, align_bytes=64)
+            yc = first.tile([P, E], BF16)
+            yc_grouped = first.tile([P, E], BF16, align_bytes=64)
+            yc_codes = first.tile([P, WO_GROUPS * P], U32, align_bytes=64)
+            yc_scales = first.tile([P, WO_GROUPS * P], U8, align_bytes=64)
+
+            nc.vector.memset(one[:], 1.0)
+            nc.scalar.sqrt(one[:], one[:])
+            nc.vector.memset(gain_rows[:], 0.0)
+            nc.vector.memset(wo_planes[:].bitcast(I32), 0)
+            nc.vector.memset(fc_planes[:].bitcast(I32), 0)
+            make_identity(nc, identity_f32[:])
+            make_identity(nc, identity_bf16[:])
+
+            for b in range(2):
+                nc.sync.dma_start(
+                    out=yc[64 * b : 64 * (b + 1), :].rearrange("t (h j) -> t h j", h=HEADS),
+                    in_=y_attn[b].rearrange("h t j -> t h j"),
+                )
+            nc.sync.dma_start(
+                out=gain_rows[0 : D // BANK, :], in_=attn_scale.rearrange("(c n) -> c n", n=BANK)
+            )
+            for g in range(WO_GROUPS):
+                load_scale_planes(
+                    nc,
+                    wo_planes[:, CHUNK * g : CHUNK * (g + 1)],
+                    wo_scale_rows[g].rearrange("q (c n) -> c q n", c=WO_BLOCKS),
+                )
+            for s in range(FC_GROUPS // PLANES_PER_TILE):
+                load_scale_planes(
+                    nc,
+                    fc_planes[:, F * s : F * (s + 1)],
+                    fc_scale_rows[PLANES_PER_TILE * s : PLANES_PER_TILE * (s + 1)],
+                )
+            wo_chunks = []
+            for c in range(WO_BLOCKS):
+                cols = slice(CHUNK * c, CHUNK * (c + 1))
+                nc.sync.dma_start(out=x_sb[:, cols], in_=x_rows[:, cols])
+                wo_chunks.append([load_chunk(nc, weights, wo_words[g, :, cols]) for g in range(WO_GROUPS)])
+            fc_chunks = [
+                load_chunk(nc, weights, fc_words[g]) for g in range(WEIGHT_SLOTS - 2 * WO_BLOCKS)
+            ]
+
+            yc_bank = banks.tile([P, BANK], F32, tag="bank")
+            transpose_pair(nc, yc_bank[:], identity_f32[:], yc[:], yc_grouped[:])
+            nc.vector.quantize_mx(
+                out=yc_codes[:].bitcast(FP8X4), scales=yc_scales[:], in_=yc_grouped[:]
+            )
+
+            for c in range(D // BANK):
+                spread = banks.tile([P, BANK], F32, tag="bank")
+                nc.tensor.matmul(
+                    out=spread[:],
+                    lhsT=identity_bf16[:, c : c + 1].to_broadcast([P, P]),
+                    rhs=gain_rows[:],
+                    start=True,
+                    stop=True,
+                )
+                if c % 2 == 0:
+                    nc.vector.tensor_copy(out=gain[:, BANK * c : BANK * (c + 1)], in_=spread[:])
+                else:
+                    nc.scalar.copy(out=gain[:, BANK * c : BANK * (c + 1)], in_=spread[:])
+
+            for c in range(WO_BLOCKS):
+                products = []
+                for j in range(BANKS_PER_CHUNK):
+                    product = banks.tile([P, BANK], F32, tag="bank")
+                    products.append(product)
+                for g in range(WO_GROUPS):
+                    for j in range(BANKS_PER_CHUNK):
+                        nc.tensor.matmul_mx(
+                            out=products[j][:],
+                            lhsT=yc_codes[:, P * g : P * (g + 1)].bitcast(FP8X4),
+                            lhsT_scale=yc_scales[:, P * g : P * (g + 1)],
+                            rhs=wo_chunks[c][g][:, BANK * j : BANK * (j + 1)].bitcast(FP8X4),
+                            rhs_scale=wo_planes[
+                                4 * c : P, CHUNK * g + BANK * j : CHUNK * g + BANK * (j + 1)
+                            ],
+                            start=(g == 0),
+                            stop=(g == WO_GROUPS - 1),
+                        )
+                for j in range(BANKS_PER_CHUNK):
+                    cols = slice(CHUNK * c + BANK * j, CHUNK * c + BANK * (j + 1))
+                    nc.vector.tensor_tensor(
+                        out=x_mid[:, cols], in0=products[j][:], in1=gain[:, cols], op=ALU.mult
+                    )
+                for j in range(BANKS_PER_CHUNK):
+                    bank_index = BANKS_PER_CHUNK * c + j
+                    cols = slice(BANK * bank_index, BANK * (bank_index + 1))
+                    nc.vector.tensor_tensor(
+                        out=x_mid[:, cols], in0=x_mid[:, cols], in1=x_sb[:, cols], op=ALU.add
+                    )
+                    squares = scratch.tile([P, BANK], BF16)
+                    nc.scalar.activation(
+                        out=squares[:],
+                        in_=x_mid[:, cols],
+                        func=ACT.Square,
+                        accum_out=sum_squares[:, bank_index : bank_index + 1],
+                    )
+                for g in range(len(fc_chunks), len(fc_chunks) + WO_GROUPS):
+                    fc_chunks.append(load_chunk(nc, weights, fc_words[g]))
+
+            for c in range(WO_BLOCKS):
+                cols = slice(CHUNK * c, CHUNK * (c + 1))
+                nc.sync.dma_start(out=x_mid_rows[:, cols], in_=x_mid[:, cols])
+
+        with tc.tile_pool(name="second", bufs=1) as second, tc.tile_pool(
+            name="positive", bufs=2
+        ) as positive, tc.psum_pool(name="flips", bufs=4) as flips, tc.psum_pool(
+            name="sums", bufs=BANKS_PER_CHUNK
+        ) as sums:
+            total = second.tile([P, 1], F32)
+            mean_square = second.tile([P, 1], F32)
+            rms = second.tile([P, 1], F32)
+            inverse_rms = second.tile([P, 1], F32)
+            xn = second.tile([P, D], BF16)
+            xn_grouped = second.tile([P, D], BF16, align_bytes=64)
+            xn_codes = second.tile([P, FC_GROUPS * P], U32, align_bytes=64)
+            xn_scales = second.tile([P, FC_GROUPS * P], U8, align_bytes=64)
+            h_sb = second.tile([P, F], F32)
+
+            nc.vector.tensor_reduce(
+                out=total[:], in_=sum_squares[:], axis=mybir.AxisListType.X, op=ALU.add
+            )
+            nc.vector.tensor_scalar(
+                out=mean_square[:],
+                in0=total[:],
+                scalar1=1.0 / D,
+                scalar2=EPS,
+                op0=ALU.mult,
+                op1=ALU.add,
+            )
+            nc.scalar.sqrt(rms[:], mean_square[:])
+            nc.vector.reciprocal(inverse_rms[:], rms[:])
+
+            for q in range(D // PAIR):
+                cols = slice(PAIR * q, PAIR * (q + 1))
+                nc.vector.tensor_scalar_mul(
+                    out=xn[:, cols], in0=x_mid[:, cols], scalar1=inverse_rms[:, 0:1]
+                )
+            for q in range(D // PAIR):
+                cols = slice(PAIR * q, PAIR * (q + 1))
+                flip_bank = flips.tile([P, BANK], F32)
+                transpose_pair(nc, flip_bank[:], identity_f32[:], xn[:, cols], xn_grouped[:, cols])
+            for q in range(D // PAIR):
+                nc.vector.quantize_mx(
+                    out=xn_codes[:, 2 * P * q : 2 * P * (q + 1)].bitcast(FP8X4),
+                    scales=xn_scales[:, 2 * P * q : 2 * P * (q + 1)],
+                    in_=xn_grouped[:, PAIR * q : PAIR * (q + 1)],
+                )
+
+            h_sums = []
+            for j in range(BANKS_PER_CHUNK):
+                h_sum = sums.tile([P, BANK], F32)
+                h_sums.append(h_sum)
+            for g in range(FC_GROUPS):
+                plane_offset = 4 * (g % PLANES_PER_TILE)
+                plane_start = F * (g // PLANES_PER_TILE)
+                for j in range(BANKS_PER_CHUNK):
+                    nc.tensor.matmul_mx(
+                        out=h_sums[j][:],
+                        lhsT=xn_codes[:, P * g : P * (g + 1)].bitcast(FP8X4),
+                        lhsT_scale=xn_scales[:, P * g : P * (g + 1)],
+                        rhs=fc_chunks[g][:, BANK * j : BANK * (j + 1)].bitcast(FP8X4),
+                        rhs_scale=fc_planes[
+                            plane_offset:P, plane_start + BANK * j : plane_start + BANK * (j + 1)
+                        ],
+                        start=(g == 0),
+                        stop=(g == FC_GROUPS - 1),
+                    )
+            for j in range(BANKS_PER_CHUNK):
+                relu = positive.tile([P, BANK], F32)
+                nc.scalar.activation(out=relu[:], in_=h_sums[j][:], func=ACT.Relu)
+                nc.vector.tensor_tensor(
+                    out=h_sb[:, BANK * j : BANK * (j + 1)], in0=relu[:], in1=relu[:], op=ALU.mult
+                )
+            nc.sync.dma_start(out=h_rows, in_=h_sb[:])

@@ -39,10 +39,10 @@ def load_chunk(nc, weights, words):
     return chunk
 
 
-def load_scale_planes(nc, planes, rows):
+def load_scale_planes(queue, word, planes, rows):
     for quad in range(P // QUADRANT):
-        nc.sync.dma_start(
-            out=planes[QUADRANT * quad : QUADRANT * quad + 16, :].bitcast(I32),
+        queue.dma_start(
+            out=planes[QUADRANT * quad : QUADRANT * quad + 16, :].bitcast(word),
             in_=rows[:, 4 * quad : 4 * quad + 4, :],
         )
 
@@ -72,7 +72,7 @@ def tile_shepherdembryo_pb_k_kernel(
     wo_words = w_o_words.rearrange("g p n t -> g p (n t)").bitcast(I32)
     fc_words = w_fc_words.rearrange("g p n t -> g p (n t)").bitcast(I32)
     wo_scale_rows = w_o_scales.bitcast(I32)
-    fc_scale_rows = w_fc_scales.bitcast(I32)
+    fc_scale_rows = w_fc_scales.bitcast(F32)
 
     with tc.manual_schedule(), tc.tile_pool(name="keep", bufs=1) as keep, tc.tile_pool(
         name="weights", bufs=WEIGHT_SLOTS
@@ -114,13 +114,15 @@ def tile_shepherdembryo_pb_k_kernel(
             )
             for g in range(WO_GROUPS):
                 load_scale_planes(
-                    nc,
+                    nc.sync,
+                    I32,
                     wo_planes[:, CHUNK * g : CHUNK * (g + 1)],
                     wo_scale_rows[g].rearrange("q (c n) -> c q n", c=WO_BLOCKS),
                 )
             for s in range(FC_GROUPS // PLANES_PER_TILE):
                 load_scale_planes(
-                    nc,
+                    nc.gpsimd,
+                    F32,
                     fc_planes[:, F * s : F * (s + 1)],
                     fc_scale_rows[PLANES_PER_TILE * s : PLANES_PER_TILE * (s + 1)],
                 )

@@ -191,10 +191,12 @@ def tile_shepherdembryo_pb_k_kernel(
                         func=ACT.Square,
                         accum_out=sum_squares[:, bank_index : bank_index + 1],
                     )
+                if c == 0:
+                    nc.gpsimd.dma_start(out=x_mid_rows[:, 0:CHUNK], in_=x_mid[:, 0:CHUNK])
                 for g in range(len(fc_chunks), len(fc_chunks) + WO_GROUPS):
                     fc_chunks.append(load_chunk(nc, weights, fc_words[g]))
 
-            for c in range(WO_BLOCKS):
+            for c in range(1, WO_BLOCKS):
                 cols = slice(CHUNK * c, CHUNK * (c + 1))
                 nc.sync.dma_start(out=x_mid_rows[:, cols], in_=x_mid[:, cols])
 

import concourse.mybir as mybir
from concourse.masks import make_identity

F32 = mybir.dt.float32
BF16 = mybir.dt.bfloat16
I32 = mybir.dt.int32
U32 = mybir.dt.uint32
U8 = mybir.dt.uint8
FP8X4 = mybir.dt.float8_e4m3fn_x4
ACT = mybir.ActivationFunctionType
ALU = mybir.AluOpType

P = 128
HEADS = 8
HEAD_DIM = 128
E = HEADS * HEAD_DIM
D = 8192
F = 2048
EPS = 1e-6

K_PASS = 512
BANK = 512
CHUNK = 2048
BANKS_PER_CHUNK = CHUNK // BANK
WO_GROUPS = E // K_PASS
FC_GROUPS = D // K_PASS
WO_BLOCKS = D // CHUNK
PAIR = 2 * K_PASS
PLANES_PER_TILE = 4
QUADRANT = 32
WEIGHT_SLOTS = 16

FLOPS = 2 * P * E * D + 2 * P * D * F


def load_chunk(nc, weights, words):
    chunk = weights.tile([P, CHUNK], U32, tag="chunk", align_bytes=64)
    nc.sync.dma_start(out=chunk[:].bitcast(I32), in_=words)
    return chunk


def load_scale_planes(queue, word, planes, rows):
    for quad in range(P // QUADRANT):
        queue.dma_start(
            out=planes[QUADRANT * quad : QUADRANT * quad + 16, :].bitcast(word),
            in_=rows[:, 4 * quad : 4 * quad + 4, :],
        )


def transpose_pair(nc, bank, identity, tokens_by_k, grouped):
    words = tokens_by_k.bitcast(F32)
    half = K_PASS // 2
    flipped = bank.rearrange("p (g u m) -> p g u m", g=2, u=2)
    for g in range(2):
        for u in range(2):
            nc.tensor.transpose(
                flipped[:, g, u, :], words[:, half * g + u : half * (g + 1) : 2], identity
            )
    nc.scalar.copy(
        out=grouped.bitcast(F32).rearrange("p (g m u) -> p g m u", g=2, u=2),
        in_=flipped.rearrange("p g u m -> p g m u"),
    )


def tile_shepherdembryo_pb_k_kernel(
    tc, y_attn, x, w_o_words, w_o_scales, attn_scale, w_fc_words, w_fc_scales, out_0, out_1
):
    nc = tc.nc
    x_rows = x.rearrange("b s d -> (b s) d")
    x_mid_rows = out_0.rearrange("b s d -> (b s) d")
    h_rows = out_1.rearrange("b s f -> (b s) f")
    wo_words = w_o_words.rearrange("g p n t -> g p (n t)").bitcast(I32)
    fc_words = w_fc_words.rearrange("g p n t -> g p (n t)").bitcast(I32)
    wo_scale_rows = w_o_scales.bitcast(I32)
    fc_scale_rows = w_fc_scales.bitcast(F32)

    with tc.manual_schedule(), tc.tile_pool(name="keep", bufs=1) as keep, tc.tile_pool(
        name="weights", bufs=WEIGHT_SLOTS
    ) as weights:
        identity_f32 = keep.tile([P, P], F32)
        x_mid = keep.tile([P, D], F32)
        sum_squares = keep.tile([P, D // BANK], F32)
        fc_planes = keep.tile([P, (FC_GROUPS // PLANES_PER_TILE) * F], U8, align_bytes=64)

        with tc.tile_pool(name="first", bufs=1) as first, tc.tile_pool(
            name="scratch", bufs=2
        ) as scratch, tc.psum_pool(name="banks", bufs=8) as banks:
            one = first.tile([P, 1], F32)
            identity_bf16 = first.tile([P, P], BF16)
            gain_rows = first.tile([P, BANK], BF16)
            gain = first.tile([P, D], BF16)
            x_sb = first.tile([P, D], BF16)
            wo_planes = first.tile([P, WO_GROUPS * CHUNK], U8, align_bytes=64)
            yc = first.tile([P, E], BF16)
            yc_grouped = first.tile([P, E], BF16, align_bytes=64)
            yc_codes = first.tile([P, WO_GROUPS * P], U32, align_bytes=64)
            yc_scales = first.tile([P, WO_GROUPS * P], U8, align_bytes=64)

            nc.vector.memset(one[:], 1.0)
            nc.scalar.sqrt(one[:], one[:])
            nc.vector.memset(gain_rows[:], 0.0)
            nc.vector.memset(wo_planes[:].bitcast(I32), 0)
            nc.vector.memset(fc_planes[:].bitcast(I32), 0)
            make_identity(nc, identity_f32[:])
            make_identity(nc, identity_bf16[:])

            for b in range(2):
                nc.sync.dma_start(
                    out=yc[64 * b : 64 * (b + 1), :].rearrange("t (h j) -> t h j", h=HEADS),
                    in_=y_attn[b].rearrange("h t j -> t h j"),
                )
            nc.sync.dma_start(
                out=gain_rows[0 : D // BANK, :], in_=attn_scale.rearrange("(c n) -> c n", n=BANK)
            )
            for g in range(WO_GROUPS):
                load_scale_planes(
                    nc.sync,
                    I32,
                    wo_planes[:, CHUNK * g : CHUNK * (g + 1)],
                    wo_scale_rows[g].rearrange("q (c n) -> c q n", c=WO_BLOCKS),
                )
            for s in range(FC_GROUPS // PLANES_PER_TILE):
                load_scale_planes(
                    nc.gpsimd,
                    F32,
                    fc_planes[:, F * s : F * (s + 1)],
                    fc_scale_rows[PLANES_PER_TILE * s : PLANES_PER_TILE * (s + 1)],
                )
            wo_chunks = []
            for c in range(WO_BLOCKS):
                cols = slice(CHUNK * c, CHUNK * (c + 1))
                nc.sync.dma_start(out=x_sb[:, cols], in_=x_rows[:, cols])
                wo_chunks.append([load_chunk(nc, weights, wo_words[g, :, cols]) for g in range(WO_GROUPS)])
            fc_chunks = [
                load_chunk(nc, weights, fc_words[g]) for g in range(WEIGHT_SLOTS - 2 * WO_BLOCKS)
            ]

            yc_bank = banks.tile([P, BANK], F32, tag="bank")
            transpose_pair(nc, yc_bank[:], identity_f32[:], yc[:], yc_grouped[:])
            nc.vector.quantize_mx(
                out=yc_codes[:].bitcast(FP8X4), scales=yc_scales[:], in_=yc_grouped[:]
            )

            for c in range(D // BANK):
                spread = banks.tile([P, BANK], F32, tag="bank")
                nc.tensor.matmul(
                    out=spread[:],
                    lhsT=identity_bf16[:, c : c + 1].to_broadcast([P, P]),
                    rhs=gain_rows[:],
                    start=True,
                    stop=True,
                )
                if c % 2 == 0:
                    nc.vector.tensor_copy(out=gain[:, BANK * c : BANK * (c + 1)], in_=spread[:])
                else:
                    nc.scalar.copy(out=gain[:, BANK * c : BANK * (c + 1)], in_=spread[:])

            for c in range(WO_BLOCKS):
                products = []
                for j in range(BANKS_PER_CHUNK):
                    product = banks.tile([P, BANK], F32, tag="bank")
                    products.append(product)
                for g in range(WO_GROUPS):
                    for j in range(BANKS_PER_CHUNK):
                        nc.tensor.matmul_mx(
                            out=products[j][:],
                            lhsT=yc_codes[:, P * g : P * (g + 1)].bitcast(FP8X4),
                            lhsT_scale=yc_scales[:, P * g : P * (g + 1)],
                            rhs=wo_chunks[c][g][:, BANK * j : BANK * (j + 1)].bitcast(FP8X4),
                            rhs_scale=wo_planes[
                                4 * c : P, CHUNK * g + BANK * j : CHUNK * g + BANK * (j + 1)
                            ],
                            start=(g == 0),
                            stop=(g == WO_GROUPS - 1),
                        )
                for j in range(BANKS_PER_CHUNK):
                    cols = slice(CHUNK * c + BANK * j, CHUNK * c + BANK * (j + 1))
                    nc.vector.tensor_tensor(
                        out=x_mid[:, cols], in0=products[j][:], in1=gain[:, cols], op=ALU.mult
                    )
                for j in range(BANKS_PER_CHUNK):
                    bank_index = BANKS_PER_CHUNK * c + j
                    cols = slice(BANK * bank_index, BANK * (bank_index + 1))
                    nc.vector.tensor_tensor(
                        out=x_mid[:, cols], in0=x_mid[:, cols], in1=x_sb[:, cols], op=ALU.add
                    )
                    squares = scratch.tile([P, BANK], BF16)
                    nc.scalar.activation(
                        out=squares[:],
                        in_=x_mid[:, cols],
                        func=ACT.Square,
                        accum_out=sum_squares[:, bank_index : bank_index + 1],
                    )
                if c == 0:
                    nc.gpsimd.dma_start(out=x_mid_rows[:, 0:CHUNK], in_=x_mid[:, 0:CHUNK])
                for g in range(len(fc_chunks), len(fc_chunks) + WO_GROUPS):
                    fc_chunks.append(load_chunk(nc, weights, fc_words[g]))

            for c in range(1, WO_BLOCKS):
                cols = slice(CHUNK * c, CHUNK * (c + 1))
                nc.sync.dma_start(out=x_mid_rows[:, cols], in_=x_mid[:, cols])

        with tc.tile_pool(name="second", bufs=1) as second, tc.tile_pool(
            name="positive", bufs=2
        ) as positive, tc.psum_pool(name="flips", bufs=4) as flips, tc.psum_pool(
            name="sums", bufs=BANKS_PER_CHUNK
        ) as sums:
            total = second.tile([P, 1], F32)
            mean_square = second.tile([P, 1], F32)
            rms = second.tile([P, 1], F32)
            inverse_rms = second.tile([P, 1], F32)
            xn = second.tile([P, D], BF16)
            xn_grouped = second.tile([P, D], BF16, align_bytes=64)
            xn_codes = second.tile([P, FC_GROUPS * P], U32, align_bytes=64)
            xn_scales = second.tile([P, FC_GROUPS * P], U8, align_bytes=64)
            h_sb = second.tile([P, F], F32)

            nc.vector.tensor_reduce(
                out=total[:], in_=sum_squares[:], axis=mybir.AxisListType.X, op=ALU.add
            )
            nc.vector.tensor_scalar(
                out=mean_square[:],
                in0=total[:],
                scalar1=1.0 / D,
                scalar2=EPS,
                op0=ALU.mult,
                op1=ALU.add,
            )
            nc.scalar.sqrt(rms[:], mean_square[:])
            nc.vector.reciprocal(inverse_rms[:], rms[:])

            for q in range(D // PAIR):
                cols = slice(PAIR * q, PAIR * (q + 1))
                nc.vector.tensor_scalar_mul(
                    out=xn[:, cols], in0=x_mid[:, cols], scalar1=inverse_rms[:, 0:1]
                )
            for q in range(D // PAIR):
                cols = slice(PAIR * q, PAIR * (q + 1))
                flip_bank = flips.tile([P, BANK], F32)
                transpose_pair(nc, flip_bank[:], identity_f32[:], xn[:, cols], xn_grouped[:, cols])
            for q in range(D // PAIR):
                nc.vector.quantize_mx(
                    out=xn_codes[:, 2 * P * q : 2 * P * (q + 1)].bitcast(FP8X4),
                    scales=xn_scales[:, 2 * P * q : 2 * P * (q + 1)],
                    in_=xn_grouped[:, PAIR * q : PAIR * (q + 1)],
                )

            h_sums = []
            for j in range(BANKS_PER_CHUNK):
                h_sum = sums.tile([P, BANK], F32)
                h_sums.append(h_sum)
            for g in range(FC_GROUPS):
                plane_offset = 4 * (g % PLANES_PER_TILE)
                plane_start = F * (g // PLANES_PER_TILE)
                for j in range(BANKS_PER_CHUNK):
                    nc.tensor.matmul_mx(
                        out=h_sums[j][:],
                        lhsT=xn_codes[:, P * g : P * (g + 1)].bitcast(FP8X4),
                        lhsT_scale=xn_scales[:, P * g : P * (g + 1)],
                        rhs=fc_chunks[g][:, BANK * j : BANK * (j + 1)].bitcast(FP8X4),
                        rhs_scale=fc_planes[
                            plane_offset:P, plane_start + BANK * j : plane_start + BANK * (j + 1)
                        ],
                        start=(g == 0),
                        stop=(g == FC_GROUPS - 1),
                    )
            for j in range(BANKS_PER_CHUNK):
                relu = positive.tile([P, BANK], F32)
                nc.scalar.activation(out=relu[:], in_=h_sums[j][:], func=ACT.Relu)
                nc.vector.tensor_tensor(
                    out=h_sb[:, BANK * j : BANK * (j + 1)], in0=relu[:], in1=relu[:], op=ALU.mult
                )
            nc.sync.dma_start(out=h_rows, in_=h_sb[:])
